import numpy as np
import ml_dtypes


def mxq(x, axis, fmt="e4m3"):
    dtype, down = {"e4m3": (ml_dtypes.float8_e4m3fn, 7), "e5m2": (ml_dtypes.float8_e5m2, 14)}[fmt]
    v = np.moveaxis(np.asarray(x, np.float32).astype(ml_dtypes.bfloat16).astype(np.float64), axis, -1)
    blocks = v.reshape(v.shape[:-1] + (-1, 32))
    amax = np.abs(blocks).max(-1, keepdims=True)
    byte = np.maximum(np.where(amax > 0, np.frexp(amax)[1] - 1 + 127, 0) - down, 1)
    scale = np.exp2(byte - 127.0)
    codes = (blocks / scale).astype(np.float32).astype(dtype).astype(np.float64)
    return np.moveaxis((codes * scale).reshape(v.shape), -1, axis)


WIDE = False


def mx_kscale(k):
    if not WIDE:
        return np.ones(k)
    levels = np.array([10, -10, 5, -5, 0])
    if k % 512:
        return np.exp2(np.random.permutation(np.resize(levels, k // 32))).repeat(32)
    a = np.empty((k // 512, 16))
    for p in range(k // 512):
        a[p, :8] = np.random.permutation(np.resize(levels, 8))
        for g in range(8):
            far = levels[np.abs(levels - a[p, g]) >= 10]
            a[p, g + 8] = far[np.random.randint(len(far))]
    return np.exp2(a.ravel()).repeat(32)


BF16 = ml_dtypes.bfloat16


def bf(x):
    return np.asarray(x, np.float32).astype(BF16)


def f64(x):
    return np.asarray(x).astype(np.float64)


B, S, F = 16, 512, 512


def stab(feature):
    var = np.var(feature, axis=2, ddof=1, keepdims=True)
    stability = 1.0 / (var + 1e-6)
    return stability / np.max(stability)


def setup_inputs():
    s = mx_kscale(S)
    s = s / s.min()
    r = np.exp2(np.random.uniform(-0.3, 0.3, (B, S, 1)))
    f0 = np.random.standard_normal((B, S, F)) * r * 2.0
    n0 = np.random.standard_normal((B, S, S)) * 3.0
    feature = bf(f0 * s[None, :, None])
    logits = n0 * stab(f64(bf(f0))) - np.log(s)[None, None, :]
    noise = bf(logits / stab(f64(feature)))
    return {"feature": feature, "noise": noise}


def reference(feature, noise):
    feature, noise = f64(feature), f64(noise)
    stability = stab(feature)
    scaled = noise * stability
    e = np.exp(scaled - scaled.max(-1, keepdims=True))
    return (mxq(e, 2, "e4m3") @ mxq(feature, 1, "e4m3")) / e.sum(-1, keepdims=True)

@@ -1,0 +1,269 @@
+from contextlib import ExitStack
+
+import concourse.mybir as mybir
+from concourse.masks import make_identity
+
+FLOPS = 2 * 16 * 512 * 512 * 512
+
+BF16 = mybir.dt.bfloat16
+F32 = mybir.dt.float32
+U32 = mybir.dt.uint32
+U8 = mybir.dt.uint8
+FP8X4 = mybir.dt.float8_e4m3fn_x4
+ALU = mybir.AluOpType
+ACT = mybir.ActivationFunctionType
+AX = mybir.AxisListType
+
+P = 128
+SEQS = 16
+Q = 4
+W = 512
+EPS = 1e-6
+STATS = 6
+
+SCALAR_VARIANCE_EVERY = 4
+GPSIMD_REGROUPS = 10
+SCALAR_REGROUPS = 15
+
+
+def weave(first, second):
+    for n in range(max(len(first), len(second))):
+        for steps in (first, second):
+            if n < len(steps):
+                steps[n]()
+
+
+def tile_frameaugment_t_kernel(tc, feature, noise, out):
+    nc = tc.nc
+    feature_quarters = feature.rearrange("b (p t) f -> b p t f", p=P)
+    noise_quarters = noise.rearrange("b (p t) j -> b p t j", p=P)
+    out_quarters = out.rearrange("b (p t) f -> b p t f", p=P)
+
+    scalar_seqs = [b for b in range(SEQS) if b % SCALAR_VARIANCE_EVERY == 1]
+    vector_seqs = [b for b in range(SEQS) if b % SCALAR_VARIANCE_EVERY != 1]
+    col = dict((b, Q * n) for n, b in enumerate(vector_seqs + scalar_seqs))
+    n_vector = Q * len(vector_seqs)
+    n_scalar = Q * len(scalar_seqs)
+
+    with ExitStack() as ctx:
+        ctx.enter_context(tc.manual_schedule())
+        keep = ctx.enter_context(tc.tile_pool(name="keep", bufs=1))
+        inputs = ctx.enter_context(tc.tile_pool(name="inputs", bufs=SEQS + SEQS - SCALAR_REGROUPS))
+        work = ctx.enter_context(tc.tile_pool(name="work", bufs=2))
+        transposed_banks = ctx.enter_context(tc.psum_pool(name="transposed_banks", bufs=4))
+        product_banks = ctx.enter_context(tc.psum_pool(name="product_banks", bufs=Q))
+
+        feature_in = []
+        for b in range(SEQS):
+            tile_in = inputs.tile([P, Q, W], BF16, name="feature_in%d" % b, tag="inputs")
+            if b < 2:
+                for t in range(Q):
+                    nc.sync.dma_start(out=tile_in[:, t, :], in_=feature_quarters[b][:, t, :])
+            else:
+                nc.sync.dma_start(out=tile_in[:], in_=feature_quarters[b])
+            feature_in.append(tile_in)
+        noise_in = []
+        for b in range(SEQS):
+            tile_in = inputs.tile([P, Q, W], BF16, name="noise_in%d" % b, tag="inputs")
+            nc.sync.dma_start(out=tile_in[:], in_=noise_quarters[b])
+            noise_in.append(tile_in)
+
+        zero = keep.tile([P, 1], F32)
+        nc.vector.memset(zero[:], 0.0)
+        one = keep.tile([P, 1], F32)
+        nc.scalar.activation(out=one[:], in_=zero[:], func=ACT.Exp)
+        identity_bf16 = keep.tile([P, P], BF16)
+        make_identity(nc, identity_bf16[:])
+        identity_f32 = keep.tile([P, P], F32)
+        make_identity(nc, identity_f32[:])
+
+        stats = keep.tile([P, n_vector, STATS], F32)
+        sums = keep.tile([P, n_scalar], F32)
+        neg_means = keep.tile([P, n_scalar], F32)
+        scalar_m2 = keep.tile([P, n_scalar], F32)
+        mean_gap = keep.tile([P, n_vector], F32)
+        gap_term = keep.tile([P, n_vector], F32)
+        m2_even_odd = keep.tile([P, n_vector], F32)
+        spread = keep.tile([P, SEQS * Q], F32)
+        inv_spread = keep.tile([P, SEQS * Q], F32)
+        stability = keep.tile([P, SEQS * Q], F32)
+        partition_min = keep.tile([P, 1], F32)
+        global_min = keep.tile([P, 1], F32)
+        row_max = [keep.tile([P, Q], F32, name="row_max%d" % b) for b in range(SEQS)]
+        exp_bias = [keep.tile([P, Q], F32, name="exp_bias%d" % b) for b in range(SEQS)]
+        row_sum = [keep.tile([P, Q], F32, name="row_sum%d" % b) for b in range(SEQS)]
+        inv_row_sum = [keep.tile([P, Q], F32, name="inv_row_sum%d" % b) for b in range(SEQS)]
+        feature_codes = [keep.tile([P, W], U32, name="feature_codes%d" % b, align_bytes=64) for b in range(SEQS)]
+        feature_scales = [keep.tile([P, W], U8, name="feature_scales%d" % b, align_bytes=64) for b in range(SEQS)]
+
+        feature_grouped = {}
+        e_rows = {}
+        e_transposed = {}
+        e_grouped = {}
+        e_quantised = {}
+        products = {}
+
+
+        def scalar_variance(b):
+            first = col[b] - n_vector
+            for t in range(Q):
+                unused = work.tile([P, W], BF16, name="unused", tag="unused")
+                nc.scalar.activation(out=unused[:], in_=feature_in[b][:, t, :], func=ACT.Copy,
+                                     accum_out=sums[:, first + t:first + t + 1])
+            nc.scalar.mul(out=neg_means[:, first:first + Q], in_=sums[:, first:first + Q], mul=-1.0 / W)
+            for t in range(Q):
+                unused = work.tile([P, W], BF16, name="unused", tag="unused")
+                nc.scalar.activation(out=unused[:], in_=feature_in[b][:, t, :], func=ACT.Square,
+                                     bias=neg_means[:, first + t:first + t + 1],
+                                     accum_out=scalar_m2[:, first + t:first + t + 1])
+
+        def regroup_feature(b):
+            grouped = work.tile([P, W, Q], BF16, name="feature_grouped", tag="feature_grouped", align_bytes=64,
+                                bufs=SCALAR_REGROUPS + 1)
+            feature_grouped[b] = grouped
+            grouped_by_fours = grouped[:].rearrange("p (c i) t -> p c t i", i=4)
+            in_by_fours = feature_in[b][:].rearrange("p t (c i) -> p c t i", i=4)
+            if b < GPSIMD_REGROUPS:
+                nc.gpsimd.tensor_scalar(out=grouped[:], in0=feature_in[b][:].rearrange("p t f -> p f t"),
+                                        scalar1=1.0, scalar2=0.0, op0=ALU.mult, op1=ALU.add)
+            elif b < SCALAR_REGROUPS:
+                nc.scalar.copy(out=grouped_by_fours, in_=in_by_fours)
+            else:
+                nc.vector.tensor_copy(out=grouped_by_fours, in_=in_by_fours)
+
+        def quantise_feature(b):
+            nc.vector.quantize_mx(out=feature_codes[b][:].bitcast(FP8X4), scales=feature_scales[b][:],
+                                  in_=feature_grouped[b][:].rearrange("p f t -> p (f t)"))
+
+        def row_max_steps(b):
+            widths = (W // 2, W // 4, W // 8, W // 16)
+            folded = [work.tile([P, Q, w], BF16, name="folded%d" % w, tag="folded%d" % w) for w in widths]
+            sources = [noise_in[b]] + folded[:-1]
+
+            def fold(n):
+                w = widths[n]
+                return lambda: nc.vector.tensor_tensor(out=folded[n][:], in0=sources[n][:, :, 0:w],
+                                                       in1=sources[n][:, :, w:2 * w], op=ALU.max)
+
+            steps = [fold(n) for n in range(len(widths))]
+            steps.append(lambda: nc.vector.tensor_reduce(out=row_max[b][:], in_=folded[-1][:], axis=AX.X, op=ALU.max))
+            return steps
+
+        def bias_of_exp(b):
+            nc.vector.scalar_tensor_tensor(out=exp_bias[b][:], in0=stability[:, col[b]:col[b] + Q], scalar=-1.0,
+                                           in1=row_max[b][:], op0=ALU.mult, op1=ALU.mult)
+
+        def exponentials(b):
+            e_rows[b] = work.tile([P, Q, W], BF16, name="e_rows", tag="e_rows")
+            for t in range(Q):
+                nc.scalar.activation(out=e_rows[b][:, t, :], in_=noise_in[b][:, t, :], func=ACT.Exp,
+                                     bias=exp_bias[b][:, t:t + 1], scale=stability[:, col[b] + t:col[b] + t + 1],
+                                     accum_out=row_sum[b][:, t:t + 1])
+
+        def transposes(b):
+            e_transposed[b] = []
+            for half in range(2):
+                bank = transposed_banks.tile([P, 2, Q, P], BF16, name="e_transposed", tag="e_transposed")
+                for u in range(2):
+                    for k in range(Q):
+                        nc.tensor.transpose(bank[:, u, k, :], e_rows[b][:, 2 * half + u, k::Q],
+                                            identity_bf16[:])
+                e_transposed[b].append(bank)
+
+        def regroup_e(b, half):
+            if half == 0:
+                e_grouped[b] = work.tile([P, Q, P, Q], BF16, name="e_grouped", tag="e_grouped", align_bytes=64)
+            nc.vector.tensor_copy(out=e_grouped[b][:, 2 * half:2 * half + 2, :, :],
+                                  in_=e_transposed[b][half][:].rearrange("p u k i -> p u i k"))
+
+        def quantise_e(b, half):
+            if half == 0:
+                e_quantised[b] = (work.tile([P, W], U32, name="e_codes", tag="e_codes", align_bytes=64),
+                                  work.tile([P, W], U8, name="e_scales", tag="e_scales", align_bytes=64))
+            codes, scales = e_quantised[b]
+            cols = slice(2 * P * half, 2 * P * (half + 1))
+            nc.vector.quantize_mx(out=codes[:, cols].bitcast(FP8X4), scales=scales[:, cols],
+                                  in_=e_grouped[b][:, 2 * half:2 * half + 2, :, :].rearrange("p u i k -> p (u i k)"))
+
+        def invert_row_sums(b):
+            nc.vector.reciprocal(out=inv_row_sum[b][:], in_=row_sum[b][:])
+
+        def multiply(b):
+            codes, scales = e_quantised[b]
+            products[b] = []
+            for t in range(Q):
+                bank = product_banks.tile([P, W], F32, name="product", tag="product")
+                nc.tensor.matmul_mx(out=bank[:], lhsT=codes[:, P * t:P * t + P].bitcast(FP8X4),
+                                    lhsT_scale=scales[:, P * t:P * t + P],
+                                    rhs=feature_codes[b][:].bitcast(FP8X4), rhs_scale=feature_scales[b][:],
+                                    start=True, stop=True)
+                products[b].append(bank)
+
+        def divide_and_store(b):
+            last = b == SEQS - 1
+            result = work.tile([P, Q, W], F32, name="result", tag="result", bufs=3)
+            for t in range(Q):
+                if last and t % 2 == 1:
+                    nc.vector.tensor_scalar(out=result[:, t, :], in0=products[b][t][:],
+                                            scalar1=inv_row_sum[b][:, t:t + 1], scalar2=None, op0=ALU.mult)
+                    nc.sync.dma_start(out=out_quarters[b][:, t - 1:t + 1, :], in_=result[:, t - 1:t + 1, :])
+                else:
+                    nc.scalar.activation(out=result[:, t, :], in_=products[b][t][:], func=ACT.Copy,
+                                         scale=inv_row_sum[b][:, t:t + 1])
+            if not last:
+                nc.sync.dma_start(out=out_quarters[b], in_=result[:])
+
+        for b in scalar_seqs:
+            scalar_variance(b)
+        for b in range(SCALAR_REGROUPS):
+            regroup_feature(b)
+        for b in vector_seqs:
+            for t in range(Q):
+                nc.vector.bn_stats(out=stats[:, col[b] + t, :], in_=feature_in[b][:, t, :])
+
+        all_minima = product_banks.tile([P, P], F32, name="all_minima", tag="product")
+        chain = [
+            lambda: nc.vector.tensor_tensor(out=mean_gap[:], in0=stats[:, :, 1], in1=stats[:, :, 4], op=ALU.subtract),
+            lambda: nc.vector.scalar_tensor_tensor(out=m2_even_odd[:], in0=stats[:, :, 2], scalar=EPS * (W - 1),
+                                                   in1=stats[:, :, 5], op0=ALU.add, op1=ALU.add),
+            lambda: nc.vector.scalar_tensor_tensor(out=gap_term[:], in0=mean_gap[:], scalar=float(W // 4),
+                                                   in1=mean_gap[:], op0=ALU.mult, op1=ALU.mult),
+            lambda: nc.vector.tensor_scalar(out=spread[:, n_vector:], in0=scalar_m2[:], scalar1=EPS * (W - 1),
+                                            scalar2=None, op0=ALU.add),
+            lambda: nc.vector.tensor_tensor(out=spread[:, 0:n_vector], in0=gap_term[:], in1=m2_even_odd[:], op=ALU.add),
+            lambda: nc.vector.tensor_reduce(out=partition_min[:], in_=spread[:], axis=AX.X, op=ALU.min),
+            lambda: nc.tensor.transpose(all_minima[:], partition_min[:].to_broadcast([P, P]), identity_f32[:]),
+            lambda: nc.vector.reciprocal(out=inv_spread[:], in_=spread[:]),
+            lambda: nc.vector.tensor_reduce(out=global_min[:], in_=all_minima[:], axis=AX.X, op=ALU.min),
+            lambda: nc.vector.tensor_scalar(out=stability[:], in0=inv_spread[:], scalar1=global_min[:, 0:1],
+                                            scalar2=None, op0=ALU.mult),
+            lambda: bias_of_exp(0),
+        ]
+        weave(chain, [step for pair in zip(row_max_steps(0), row_max_steps(1)) for step in pair])
+        bias_of_exp(1)
+
+        for i in range(-2, SEQS + 1):
+            if i + 2 < SEQS:
+                exponentials(i + 2)
+            if 0 <= i + 1 < SEQS:
+                transposes(i + 1)
+            if i >= 1:
+                multiply(i - 1)
+            maxima = row_max_steps(i + 3) if 2 <= i + 3 < SEQS else []
+            others = []
+            if 0 <= i < SEQS:
+                others.append(lambda: regroup_e(i, 0))
+                others.append(lambda: regroup_e(i, 1))
+            if 0 <= i + 1 < SEQS:
+                others.append(lambda: quantise_feature(i + 1))
+            if SCALAR_REGROUPS <= i + 3 < SEQS:
+                others.append(lambda: regroup_feature(i + 3))
+            if 0 <= i < SEQS:
+                others.append(lambda: quantise_e(i, 0))
+                others.append(lambda: quantise_e(i, 1))
+                others.append(lambda: invert_row_sums(i))
+            weave(maxima, others)
+            if maxima:
+                bias_of_exp(i + 3)
+            if i >= 1:
+                divide_and_store(i - 1)

@@ -21,9 +21,10 @@ W = 512
 EPS = 1e-6
 STATS = 6
 
-SCALAR_VARIANCE_EVERY = 4
+SCALAR_VARIANCE_EVERY = 3
+VECTOR_DIVIDES_EVERY = 2
 GPSIMD_REGROUPS = 10
-SCALAR_REGROUPS = 15
+SCALAR_REGROUPS = 11
 
 
 def weave(first, second):
@@ -53,15 +54,12 @@ def tile_frameaugment_t_kernel(tc, feature, noise, out):
         transposed_banks = ctx.enter_context(tc.psum_pool(name="transposed_banks", bufs=4))
         product_banks = ctx.enter_context(tc.psum_pool(name="product_banks", bufs=Q))
 
-        feature_in = []
-        for b in range(SEQS):
-            tile_in = inputs.tile([P, Q, W], BF16, name="feature_in%d" % b, tag="inputs")
-            if b < 2:
-                for t in range(Q):
-                    nc.sync.dma_start(out=tile_in[:, t, :], in_=feature_quarters[b][:, t, :])
-            else:
-                nc.sync.dma_start(out=tile_in[:], in_=feature_quarters[b])
-            feature_in.append(tile_in)
+        feature_in = [inputs.tile([P, Q, W], BF16, name="feature_in%d" % b, tag="inputs") for b in range(SEQS)]
+        for t in range(Q):
+            for b in range(2):
+                nc.sync.dma_start(out=feature_in[b][:, t, :], in_=feature_quarters[b][:, t, :])
+        for b in range(2, SEQS):
+            nc.sync.dma_start(out=feature_in[b][:], in_=feature_quarters[b])
         noise_in = []
         for b in range(SEQS):
             tile_in = inputs.tile([P, Q, W], BF16, name="noise_in%d" % b, tag="inputs")
@@ -72,8 +70,6 @@ def tile_frameaugment_t_kernel(tc, feature, noise, out):
         nc.vector.memset(zero[:], 0.0)
         one = keep.tile([P, 1], F32)
         nc.scalar.activation(out=one[:], in_=zero[:], func=ACT.Exp)
-        identity_bf16 = keep.tile([P, P], BF16)
-        make_identity(nc, identity_bf16[:])
         identity_f32 = keep.tile([P, P], F32)
         make_identity(nc, identity_f32[:])
 
@@ -156,25 +152,29 @@ def tile_frameaugment_t_kernel(tc, feature, noise, out):
         def exponentials(b):
             e_rows[b] = work.tile([P, Q, W], BF16, name="e_rows", tag="e_rows")
             for t in range(Q):
-                nc.scalar.activation(out=e_rows[b][:, t, :], in_=noise_in[b][:, t, :], func=ACT.Exp,
+                nc.scalar.activation(out=e_rows[b][:, t, :].rearrange("p (u w h) -> p u w h", u=2, h=2),
+                                     in_=noise_in[b][:, t, :].rearrange("p (w u h) -> p u w h", u=2, h=2), func=ACT.Exp,
                                      bias=exp_bias[b][:, t:t + 1], scale=stability[:, col[b] + t:col[b] + t + 1],
                                      accum_out=row_sum[b][:, t:t + 1])
 
         def transposes(b):
+            words = e_rows[b][:].rearrange("p t j -> p (t j)").bitcast(F32)
             e_transposed[b] = []
             for half in range(2):
-                bank = transposed_banks.tile([P, 2, Q, P], BF16, name="e_transposed", tag="e_transposed")
-                for u in range(2):
-                    for k in range(Q):
-                        nc.tensor.transpose(bank[:, u, k, :], e_rows[b][:, 2 * half + u, k::Q],
-                                            identity_bf16[:])
+                bank = transposed_banks.tile([P, 2, 2, P], F32, name="e_transposed", tag="e_transposed")
+                for v in range(2):
+                    for u in range(2):
+                        run = (2 * half + v) * 2 + u
+                        nc.tensor.transpose(bank[:, v, u, :], words[:, P * run:P * run + P], identity_f32[:])
                 e_transposed[b].append(bank)
 
         def regroup_e(b, half):
             if half == 0:
                 e_grouped[b] = work.tile([P, Q, P, Q], BF16, name="e_grouped", tag="e_grouped", align_bytes=64)
-            nc.vector.tensor_copy(out=e_grouped[b][:, 2 * half:2 * half + 2, :, :],
-                                  in_=e_transposed[b][half][:].rearrange("p u k i -> p u i k"))
+            words = e_grouped[b][:].rearrange("p t i k -> p (t i k)").bitcast(F32)
+            words = words.rearrange("p (t i u) -> p t i u", t=Q, u=2)
+            nc.vector.tensor_copy(out=words[:, 2 * half:2 * half + 2, :, :],
+                                  in_=e_transposed[b][half][:].rearrange("p v u i -> p v i u"))
 
         def quantise_e(b, half):
             if half == 0:
@@ -203,13 +203,15 @@ def tile_frameaugment_t_kernel(tc, feature, noise, out):
             last = b == SEQS - 1
             result = work.tile([P, Q, W], F32, name="result", tag="result", bufs=3)
             for t in range(Q):
-                if last and t % 2 == 1:
+                vectors = t % 2 == 1 if last else b % VECTOR_DIVIDES_EVERY == 1 and t == Q - 1
+                if vectors:
                     nc.vector.tensor_scalar(out=result[:, t, :], in0=products[b][t][:],
                                             scalar1=inv_row_sum[b][:, t:t + 1], scalar2=None, op0=ALU.mult)
-                    nc.sync.dma_start(out=out_quarters[b][:, t - 1:t + 1, :], in_=result[:, t - 1:t + 1, :])
                 else:
                     nc.scalar.activation(out=result[:, t, :], in_=products[b][t][:], func=ACT.Copy,
                                          scale=inv_row_sum[b][:, t:t + 1])
+                if last and t % 2 == 1:
+                    nc.sync.dma_start(out=out_quarters[b][:, t - 1:t + 1, :], in_=result[:, t - 1:t + 1, :])
             if not last:
                 nc.sync.dma_start(out=out_quarters[b], in_=result[:])
 

@@ -21,10 +21,10 @@ W = 512
 EPS = 1e-6
 STATS = 6
 
-SCALAR_VARIANCE_EVERY = 3
-VECTOR_DIVIDES_EVERY = 2
-GPSIMD_REGROUPS = 10
-SCALAR_REGROUPS = 11
+VECTOR_VARIANCES = 3
+GPSIMD_REGROUPS = 9
+SCALAR_REGROUPS = 13
+VECTOR_DIVIDES_NOT = 4
 
 
 def weave(first, second):
@@ -40,12 +40,6 @@ def tile_frameaugment_t_kernel(tc, feature, noise, out):
     noise_quarters = noise.rearrange("b (p t) j -> b p t j", p=P)
     out_quarters = out.rearrange("b (p t) f -> b p t f", p=P)
 
-    scalar_seqs = [b for b in range(SEQS) if b % SCALAR_VARIANCE_EVERY == 1]
-    vector_seqs = [b for b in range(SEQS) if b % SCALAR_VARIANCE_EVERY != 1]
-    col = dict((b, Q * n) for n, b in enumerate(vector_seqs + scalar_seqs))
-    n_vector = Q * len(vector_seqs)
-    n_scalar = Q * len(scalar_seqs)
-
     with ExitStack() as ctx:
         ctx.enter_context(tc.manual_schedule())
         keep = ctx.enter_context(tc.tile_pool(name="keep", bufs=1))
@@ -55,10 +49,9 @@ def tile_frameaugment_t_kernel(tc, feature, noise, out):
         product_banks = ctx.enter_context(tc.psum_pool(name="product_banks", bufs=Q))
 
         feature_in = [inputs.tile([P, Q, W], BF16, name="feature_in%d" % b, tag="inputs") for b in range(SEQS)]
-        for t in range(Q):
-            for b in range(2):
-                nc.sync.dma_start(out=feature_in[b][:, t, :], in_=feature_quarters[b][:, t, :])
-        for b in range(2, SEQS):
+        for t in (0, Q - 1, 1, 2):
+            nc.sync.dma_start(out=feature_in[0][:, t, :], in_=feature_quarters[0][:, t, :])
+        for b in range(1, SEQS):
             nc.sync.dma_start(out=feature_in[b][:], in_=feature_quarters[b])
         noise_in = []
         for b in range(SEQS):
@@ -73,20 +66,19 @@ def tile_frameaugment_t_kernel(tc, feature, noise, out):
         identity_f32 = keep.tile([P, P], F32)
         make_identity(nc, identity_f32[:])
 
-        stats = keep.tile([P, n_vector, STATS], F32)
-        sums = keep.tile([P, n_scalar], F32)
-        neg_means = keep.tile([P, n_scalar], F32)
-        scalar_m2 = keep.tile([P, n_scalar], F32)
-        mean_gap = keep.tile([P, n_vector], F32)
-        gap_term = keep.tile([P, n_vector], F32)
-        m2_even_odd = keep.tile([P, n_vector], F32)
-        spread = keep.tile([P, SEQS * Q], F32)
-        inv_spread = keep.tile([P, SEQS * Q], F32)
-        stability = keep.tile([P, SEQS * Q], F32)
+        stats = keep.tile([P, SEQS, VECTOR_VARIANCES, STATS], F32)
+        neg_means = keep.tile([P, SEQS], F32)
+        scalar_m2 = keep.tile([P, SEQS], F32)
+        mean_gap = keep.tile([P, SEQS, VECTOR_VARIANCES], F32)
+        gap_term = keep.tile([P, SEQS, VECTOR_VARIANCES], F32)
+        m2_even_odd = keep.tile([P, SEQS, VECTOR_VARIANCES], F32)
+        spread = keep.tile([P, SEQS, Q], F32)
+        inv_spread = keep.tile([P, SEQS, Q], F32)
+        stability = keep.tile([P, SEQS, Q], F32)
         partition_min = keep.tile([P, 1], F32)
         global_min = keep.tile([P, 1], F32)
-        row_max = [keep.tile([P, Q], F32, name="row_max%d" % b) for b in range(SEQS)]
-        exp_bias = [keep.tile([P, Q], F32, name="exp_bias%d" % b) for b in range(SEQS)]
+        row_max = [keep.tile([P, 2, Q], F32, name="row_max%d" % n) for n in range(SEQS // 2)]
+        exp_bias = [keep.tile([P, 2, Q], F32, name="exp_bias%d" % n) for n in range(SEQS // 2)]
         row_sum = [keep.tile([P, Q], F32, name="row_sum%d" % b) for b in range(SEQS)]
         inv_row_sum = [keep.tile([P, Q], F32, name="inv_row_sum%d" % b) for b in range(SEQS)]
         feature_codes = [keep.tile([P, W], U32, name="feature_codes%d" % b, align_bytes=64) for b in range(SEQS)]
@@ -100,22 +92,19 @@ def tile_frameaugment_t_kernel(tc, feature, noise, out):
         products = {}
 
 
-        def scalar_variance(b):
-            first = col[b] - n_vector
-            for t in range(Q):
-                unused = work.tile([P, W], BF16, name="unused", tag="unused")
-                nc.scalar.activation(out=unused[:], in_=feature_in[b][:, t, :], func=ACT.Copy,
-                                     accum_out=sums[:, first + t:first + t + 1])
-            nc.scalar.mul(out=neg_means[:, first:first + Q], in_=sums[:, first:first + Q], mul=-1.0 / W)
-            for t in range(Q):
-                unused = work.tile([P, W], BF16, name="unused", tag="unused")
-                nc.scalar.activation(out=unused[:], in_=feature_in[b][:, t, :], func=ACT.Square,
-                                     bias=neg_means[:, first + t:first + t + 1],
-                                     accum_out=scalar_m2[:, first + t:first + t + 1])
+        def scalar_mean(b):
+            unused = work.tile([P, W], BF16, name="unused", tag="unused")
+            nc.scalar.activation(out=unused[:], in_=feature_in[b][:, VECTOR_VARIANCES, :], func=ACT.Copy,
+                                 scale=-1.0 / W, accum_out=neg_means[:, b:b + 1])
+
+        def scalar_squares(b):
+            unused = work.tile([P, W], BF16, name="unused", tag="unused")
+            nc.scalar.activation(out=unused[:], in_=feature_in[b][:, VECTOR_VARIANCES, :], func=ACT.Square,
+                                 bias=neg_means[:, b:b + 1], accum_out=scalar_m2[:, b:b + 1])
 
         def regroup_feature(b):
             grouped = work.tile([P, W, Q], BF16, name="feature_grouped", tag="feature_grouped", align_bytes=64,
-                                bufs=SCALAR_REGROUPS + 1)
+                                bufs=SCALAR_REGROUPS)
             feature_grouped[b] = grouped
             grouped_by_fours = grouped[:].rearrange("p (c i) t -> p c t i", i=4)
             in_by_fours = feature_in[b][:].rearrange("p t (c i) -> p c t i", i=4)
@@ -131,30 +120,36 @@ def tile_frameaugment_t_kernel(tc, feature, noise, out):
             nc.vector.quantize_mx(out=feature_codes[b][:].bitcast(FP8X4), scales=feature_scales[b][:],
                                   in_=feature_grouped[b][:].rearrange("p f t -> p (f t)"))
 
-        def row_max_steps(b):
+        def row_max_steps(n):
             widths = (W // 2, W // 4, W // 8, W // 16)
-            folded = [work.tile([P, Q, w], BF16, name="folded%d" % w, tag="folded%d" % w) for w in widths]
-            sources = [noise_in[b]] + folded[:-1]
+            folded = [work.tile([P, 2, Q, w], BF16, name="folded%d" % w, tag="folded%d" % w) for w in widths]
 
-            def fold(n):
-                w = widths[n]
-                return lambda: nc.vector.tensor_tensor(out=folded[n][:], in0=sources[n][:, :, 0:w],
-                                                       in1=sources[n][:, :, w:2 * w], op=ALU.max)
+            def first_fold(s):
+                w = widths[0]
+                source = noise_in[2 * n + s]
+                return lambda: nc.vector.tensor_tensor(out=folded[0][:, s, :, :], in0=source[:, :, 0:w],
+                                                       in1=source[:, :, w:2 * w], op=ALU.max)
 
-            steps = [fold(n) for n in range(len(widths))]
-            steps.append(lambda: nc.vector.tensor_reduce(out=row_max[b][:], in_=folded[-1][:], axis=AX.X, op=ALU.max))
+            def fold(m):
+                w = widths[m]
+                both = [folded[m - 1][:].rearrange("p s t w -> p (s t) w"), folded[m][:].rearrange("p s t w -> p (s t) w")]
+                return lambda: nc.vector.tensor_tensor(out=both[1], in0=both[0][:, :, 0:w],
+                                                       in1=both[0][:, :, w:2 * w], op=ALU.max)
+
+            steps = [first_fold(0), first_fold(1)]
+            steps.extend([fold(m) for m in range(1, len(widths))])
+            steps.append(lambda: nc.vector.tensor_reduce(out=row_max[n][:], in_=folded[-1][:], axis=AX.X, op=ALU.max))
+            steps.append(lambda: nc.vector.scalar_tensor_tensor(
+                out=exp_bias[n][:], in0=stability[:, 2 * n:2 * n + 2, :], scalar=-1.0, in1=row_max[n][:],
+                op0=ALU.mult, op1=ALU.mult))
             return steps
-
-        def bias_of_exp(b):
-            nc.vector.scalar_tensor_tensor(out=exp_bias[b][:], in0=stability[:, col[b]:col[b] + Q], scalar=-1.0,
-                                           in1=row_max[b][:], op0=ALU.mult, op1=ALU.mult)
 
         def exponentials(b):
             e_rows[b] = work.tile([P, Q, W], BF16, name="e_rows", tag="e_rows")
             for t in range(Q):
                 nc.scalar.activation(out=e_rows[b][:, t, :].rearrange("p (u w h) -> p u w h", u=2, h=2),
                                      in_=noise_in[b][:, t, :].rearrange("p (w u h) -> p u w h", u=2, h=2), func=ACT.Exp,
-                                     bias=exp_bias[b][:, t:t + 1], scale=stability[:, col[b] + t:col[b] + t + 1],
+                                     bias=exp_bias[b // 2][:, b % 2, t:t + 1], scale=stability[:, b, t:t + 1],
                                      accum_out=row_sum[b][:, t:t + 1])
 
         def transposes(b):
@@ -176,14 +171,12 @@ def tile_frameaugment_t_kernel(tc, feature, noise, out):
             nc.vector.tensor_copy(out=words[:, 2 * half:2 * half + 2, :, :],
                                   in_=e_transposed[b][half][:].rearrange("p v u i -> p v i u"))
 
-        def quantise_e(b, half):
-            if half == 0:
-                e_quantised[b] = (work.tile([P, W], U32, name="e_codes", tag="e_codes", align_bytes=64),
-                                  work.tile([P, W], U8, name="e_scales", tag="e_scales", align_bytes=64))
-            codes, scales = e_quantised[b]
-            cols = slice(2 * P * half, 2 * P * (half + 1))
-            nc.vector.quantize_mx(out=codes[:, cols].bitcast(FP8X4), scales=scales[:, cols],
-                                  in_=e_grouped[b][:, 2 * half:2 * half + 2, :, :].rearrange("p u i k -> p (u i k)"))
+        def quantise_e(b):
+            codes = work.tile([P, W], U32, name="e_codes", tag="e_codes", align_bytes=64)
+            scales = work.tile([P, W], U8, name="e_scales", tag="e_scales", align_bytes=64)
+            e_quantised[b] = (codes, scales)
+            nc.vector.quantize_mx(out=codes[:].bitcast(FP8X4), scales=scales[:],
+                                  in_=e_grouped[b][:].rearrange("p t i k -> p (t i k)"))
 
         def invert_row_sums(b):
             nc.vector.reciprocal(out=inv_row_sum[b][:], in_=row_sum[b][:])
@@ -203,7 +196,7 @@ def tile_frameaugment_t_kernel(tc, feature, noise, out):
             last = b == SEQS - 1
             result = work.tile([P, Q, W], F32, name="result", tag="result", bufs=3)
             for t in range(Q):
-                vectors = t % 2 == 1 if last else b % VECTOR_DIVIDES_EVERY == 1 and t == Q - 1
+                vectors = t % 2 == 1 if last else b % VECTOR_DIVIDES_NOT > 0 and t == Q - 1
                 if vectors:
                     nc.vector.tensor_scalar(out=result[:, t, :], in0=products[b][t][:],
                                             scalar1=inv_row_sum[b][:, t:t + 1], scalar2=None, op0=ALU.mult)
@@ -215,35 +208,40 @@ def tile_frameaugment_t_kernel(tc, feature, noise, out):
             if not last:
                 nc.sync.dma_start(out=out_quarters[b], in_=result[:])
 
-        for b in scalar_seqs:
-            scalar_variance(b)
+        for b in range(SEQS + 1):
+            if b < SEQS:
+                scalar_mean(b)
+            if b >= 1:
+                scalar_squares(b - 1)
         for b in range(SCALAR_REGROUPS):
             regroup_feature(b)
-        for b in vector_seqs:
-            for t in range(Q):
-                nc.vector.bn_stats(out=stats[:, col[b] + t, :], in_=feature_in[b][:, t, :])
+        for b in range(SEQS):
+            for t in range(VECTOR_VARIANCES):
+                nc.vector.bn_stats(out=stats[:, b, t, :], in_=feature_in[b][:, t, :])
 
         all_minima = product_banks.tile([P, P], F32, name="all_minima", tag="product")
         chain = [
-            lambda: nc.vector.tensor_tensor(out=mean_gap[:], in0=stats[:, :, 1], in1=stats[:, :, 4], op=ALU.subtract),
-            lambda: nc.vector.scalar_tensor_tensor(out=m2_even_odd[:], in0=stats[:, :, 2], scalar=EPS * (W - 1),
-                                                   in1=stats[:, :, 5], op0=ALU.add, op1=ALU.add),
+            lambda: nc.vector.tensor_tensor(out=mean_gap[:], in0=stats[:, :, :, 1], in1=stats[:, :, :, 4], op=ALU.subtract),
+            lambda: nc.vector.scalar_tensor_tensor(out=m2_even_odd[:], in0=stats[:, :, :, 2], scalar=EPS * (W - 1),
+                                                   in1=stats[:, :, :, 5], op0=ALU.add, op1=ALU.add),
             lambda: nc.vector.scalar_tensor_tensor(out=gap_term[:], in0=mean_gap[:], scalar=float(W // 4),
                                                    in1=mean_gap[:], op0=ALU.mult, op1=ALU.mult),
-            lambda: nc.vector.tensor_scalar(out=spread[:, n_vector:], in0=scalar_m2[:], scalar1=EPS * (W - 1),
+            lambda: nc.vector.tensor_scalar(out=spread[:, :, VECTOR_VARIANCES], in0=scalar_m2[:], scalar1=EPS * (W - 1),
                                             scalar2=None, op0=ALU.add),
-            lambda: nc.vector.tensor_tensor(out=spread[:, 0:n_vector], in0=gap_term[:], in1=m2_even_odd[:], op=ALU.add),
-            lambda: nc.vector.tensor_reduce(out=partition_min[:], in_=spread[:], axis=AX.X, op=ALU.min),
+            lambda: nc.vector.tensor_tensor(out=spread[:, :, 0:VECTOR_VARIANCES], in0=gap_term[:], in1=m2_even_odd[:],
+                                            op=ALU.add),
+            lambda: nc.vector.tensor_reduce(out=partition_min[:], in_=spread[:], axis=AX.XY, op=ALU.min),
             lambda: nc.tensor.transpose(all_minima[:], partition_min[:].to_broadcast([P, P]), identity_f32[:]),
             lambda: nc.vector.reciprocal(out=inv_spread[:], in_=spread[:]),
             lambda: nc.vector.tensor_reduce(out=global_min[:], in_=all_minima[:], axis=AX.X, op=ALU.min),
             lambda: nc.vector.tensor_scalar(out=stability[:], in0=inv_spread[:], scalar1=global_min[:, 0:1],
                                             scalar2=None, op0=ALU.mult),
-            lambda: bias_of_exp(0),
         ]
-        weave(chain, [step for pair in zip(row_max_steps(0), row_max_steps(1)) for step in pair])
-        bias_of_exp(1)
+        first_maxima = row_max_steps(0)
+        weave(chain, first_maxima[:-1])
+        first_maxima[-1]()
 
+        maxima = []
         for i in range(-2, SEQS + 1):
             if i + 2 < SEQS:
                 exponentials(i + 2)
@@ -251,21 +249,22 @@ def tile_frameaugment_t_kernel(tc, feature, noise, out):
                 transposes(i + 1)
             if i >= 1:
                 multiply(i - 1)
-            maxima = row_max_steps(i + 3) if 2 <= i + 3 < SEQS else []
+            if i % 2 == 0:
+                steps = row_max_steps(i // 2 + 2) if i + 4 < SEQS else []
+                maxima, later = steps[:3], steps[3:]
+            else:
+                maxima = later
             others = []
             if 0 <= i < SEQS:
                 others.append(lambda: regroup_e(i, 0))
                 others.append(lambda: regroup_e(i, 1))
             if 0 <= i + 1 < SEQS:
                 others.append(lambda: quantise_feature(i + 1))
+            if 0 <= i < SEQS:
+                others.append(lambda: quantise_e(i))
+                others.append(lambda: invert_row_sums(i))
             if SCALAR_REGROUPS <= i + 3 < SEQS:
                 others.append(lambda: regroup_feature(i + 3))
-            if 0 <= i < SEQS:
-                others.append(lambda: quantise_e(i, 0))
-                others.append(lambda: quantise_e(i, 1))
-                others.append(lambda: invert_row_sums(i))
             weave(maxima, others)
-            if maxima:
-                bias_of_exp(i + 3)
             if i >= 1:
                 divide_and_store(i - 1)

@@ -22,8 +22,9 @@ EPS = 1e-6
 STATS = 6
 
 VECTOR_VARIANCES = 3
+SCALAR_TAKES_TWO = 12
 GPSIMD_REGROUPS = 9
-SCALAR_REGROUPS = 13
+TENSOR_REGROUPS = 14
 VECTOR_DIVIDES_NOT = 4
 
 
@@ -43,7 +44,7 @@ def tile_frameaugment_t_kernel(tc, feature, noise, out):
     with ExitStack() as ctx:
         ctx.enter_context(tc.manual_schedule())
         keep = ctx.enter_context(tc.tile_pool(name="keep", bufs=1))
-        inputs = ctx.enter_context(tc.tile_pool(name="inputs", bufs=SEQS + SEQS - SCALAR_REGROUPS))
+        inputs = ctx.enter_context(tc.tile_pool(name="inputs", bufs=SEQS + SEQS - TENSOR_REGROUPS))
         work = ctx.enter_context(tc.tile_pool(name="work", bufs=2))
         transposed_banks = ctx.enter_context(tc.psum_pool(name="transposed_banks", bufs=4))
         product_banks = ctx.enter_context(tc.psum_pool(name="product_banks", bufs=Q))
@@ -65,10 +66,12 @@ def tile_frameaugment_t_kernel(tc, feature, noise, out):
         nc.scalar.activation(out=one[:], in_=zero[:], func=ACT.Exp)
         identity_f32 = keep.tile([P, P], F32)
         make_identity(nc, identity_f32[:])
+        identity_bf16 = keep.tile([P, P], BF16)
+        make_identity(nc, identity_bf16[:])
 
         stats = keep.tile([P, SEQS, VECTOR_VARIANCES, STATS], F32)
-        neg_means = keep.tile([P, SEQS], F32)
-        scalar_m2 = keep.tile([P, SEQS], F32)
+        neg_means = keep.tile([P, SEQS, 2], F32)
+        scalar_m2 = keep.tile([P, SEQS, 2], F32)
         mean_gap = keep.tile([P, SEQS, VECTOR_VARIANCES], F32)
         gap_term = keep.tile([P, SEQS, VECTOR_VARIANCES], F32)
         m2_even_odd = keep.tile([P, SEQS, VECTOR_VARIANCES], F32)
@@ -79,8 +82,8 @@ def tile_frameaugment_t_kernel(tc, feature, noise, out):
         global_min = keep.tile([P, 1], F32)
         row_max = [keep.tile([P, 2, Q], F32, name="row_max%d" % n) for n in range(SEQS // 2)]
         exp_bias = [keep.tile([P, 2, Q], F32, name="exp_bias%d" % n) for n in range(SEQS // 2)]
-        row_sum = [keep.tile([P, Q], F32, name="row_sum%d" % b) for b in range(SEQS)]
-        inv_row_sum = [keep.tile([P, Q], F32, name="inv_row_sum%d" % b) for b in range(SEQS)]
+        row_sum = [keep.tile([P, 2, Q], F32, name="row_sum%d" % n) for n in range(SEQS // 2)]
+        inv_row_sum = [keep.tile([P, 2, Q], F32, name="inv_row_sum%d" % n) for n in range(SEQS // 2)]
         feature_codes = [keep.tile([P, W], U32, name="feature_codes%d" % b, align_bytes=64) for b in range(SEQS)]
         feature_scales = [keep.tile([P, W], U8, name="feature_scales%d" % b, align_bytes=64) for b in range(SEQS)]
 
@@ -92,29 +95,35 @@ def tile_frameaugment_t_kernel(tc, feature, noise, out):
         products = {}
 
 
-        def scalar_mean(b):
+        def scalar_mean(b, t):
             unused = work.tile([P, W], BF16, name="unused", tag="unused")
-            nc.scalar.activation(out=unused[:], in_=feature_in[b][:, VECTOR_VARIANCES, :], func=ACT.Copy,
-                                 scale=-1.0 / W, accum_out=neg_means[:, b:b + 1])
+            nc.scalar.activation(out=unused[:], in_=feature_in[b][:, t, :], func=ACT.Copy,
+                                 scale=-1.0 / W, accum_out=neg_means[:, b, t - 2:t - 1])
 
-        def scalar_squares(b):
+        def scalar_squares(b, t):
             unused = work.tile([P, W], BF16, name="unused", tag="unused")
-            nc.scalar.activation(out=unused[:], in_=feature_in[b][:, VECTOR_VARIANCES, :], func=ACT.Square,
-                                 bias=neg_means[:, b:b + 1], accum_out=scalar_m2[:, b:b + 1])
+            nc.scalar.activation(out=unused[:], in_=feature_in[b][:, t, :], func=ACT.Square,
+                                 bias=neg_means[:, b, t - 2:t - 1], accum_out=scalar_m2[:, b, t - 2:t - 1])
 
         def regroup_feature(b):
             grouped = work.tile([P, W, Q], BF16, name="feature_grouped", tag="feature_grouped", align_bytes=64,
-                                bufs=SCALAR_REGROUPS)
+                                bufs=TENSOR_REGROUPS)
             feature_grouped[b] = grouped
-            grouped_by_fours = grouped[:].rearrange("p (c i) t -> p c t i", i=4)
-            in_by_fours = feature_in[b][:].rearrange("p t (c i) -> p c t i", i=4)
             if b < GPSIMD_REGROUPS:
                 nc.gpsimd.tensor_scalar(out=grouped[:], in0=feature_in[b][:].rearrange("p t f -> p f t"),
                                         scalar1=1.0, scalar2=0.0, op0=ALU.mult, op1=ALU.add)
-            elif b < SCALAR_REGROUPS:
-                nc.scalar.copy(out=grouped_by_fours, in_=in_by_fours)
+            elif b < TENSOR_REGROUPS:
+                for half, pool, tag in ((0, transposed_banks, "e_transposed"), (1, product_banks, "product")):
+                    cols = slice(W // 2 * half, W // 2 * (half + 1))
+                    bank = pool.tile([P, W // 2, Q], BF16, name="regrouped", tag=tag)
+                    for n in range(2):
+                        nc.tensor.matmul(bank[:, P * n:P * n + P, :], lhsT=identity_bf16[:],
+                                         rhs=feature_in[b][:, :, P * (2 * half + n):P * (2 * half + n + 1)].rearrange("p k f -> p f k"),
+                                         start=True, stop=True)
+                    nc.scalar.copy(out=grouped[:, cols, :], in_=bank[:])
             else:
-                nc.vector.tensor_copy(out=grouped_by_fours, in_=in_by_fours)
+                nc.vector.tensor_copy(out=grouped[:].rearrange("p (c i) t -> p c t i", i=4),
+                                      in_=feature_in[b][:].rearrange("p t (c i) -> p c t i", i=4))
 
         def quantise_feature(b):
             nc.vector.quantize_mx(out=feature_codes[b][:].bitcast(FP8X4), scales=feature_scales[b][:],
@@ -150,7 +159,7 @@ def tile_frameaugment_t_kernel(tc, feature, noise, out):
                 nc.scalar.activation(out=e_rows[b][:, t, :].rearrange("p (u w h) -> p u w h", u=2, h=2),
                                      in_=noise_in[b][:, t, :].rearrange("p (w u h) -> p u w h", u=2, h=2), func=ACT.Exp,
                                      bias=exp_bias[b // 2][:, b % 2, t:t + 1], scale=stability[:, b, t:t + 1],
-                                     accum_out=row_sum[b][:, t:t + 1])
+                                     accum_out=row_sum[b // 2][:, b % 2, t:t + 1])
 
         def transposes(b):
             words = e_rows[b][:].rearrange("p t j -> p (t j)").bitcast(F32)
@@ -178,8 +187,8 @@ def tile_frameaugment_t_kernel(tc, feature, noise, out):
             nc.vector.quantize_mx(out=codes[:].bitcast(FP8X4), scales=scales[:],
                                   in_=e_grouped[b][:].rearrange("p t i k -> p (t i k)"))
 
-        def invert_row_sums(b):
-            nc.vector.reciprocal(out=inv_row_sum[b][:], in_=row_sum[b][:])
+        def invert_row_sums(n):
+            nc.vector.reciprocal(out=inv_row_sum[n][:], in_=row_sum[n][:])
 
         def multiply(b):
             codes, scales = e_quantised[b]
@@ -194,52 +203,62 @@ def tile_frameaugment_t_kernel(tc, feature, noise, out):
 
         def divide_and_store(b):
             last = b == SEQS - 1
-            result = work.tile([P, Q, W], F32, name="result", tag="result", bufs=3)
-            for t in range(Q):
-                vectors = t % 2 == 1 if last else b % VECTOR_DIVIDES_NOT > 0 and t == Q - 1
-                if vectors:
-                    nc.vector.tensor_scalar(out=result[:, t, :], in0=products[b][t][:],
-                                            scalar1=inv_row_sum[b][:, t:t + 1], scalar2=None, op0=ALU.mult)
-                else:
-                    nc.scalar.activation(out=result[:, t, :], in_=products[b][t][:], func=ACT.Copy,
-                                         scale=inv_row_sum[b][:, t:t + 1])
-                if last and t % 2 == 1:
-                    nc.sync.dma_start(out=out_quarters[b][:, t - 1:t + 1, :], in_=result[:, t - 1:t + 1, :])
-            if not last:
-                nc.sync.dma_start(out=out_quarters[b], in_=result[:])
+            for half in range(2):
+                result = work.tile([P, 2, W], F32, name="result", tag="result", bufs=6)
+                for v in range(2):
+                    t = 2 * half + v
+                    scale = inv_row_sum[b // 2][:, b % 2, t:t + 1]
+                    if v == 1 if last else b % VECTOR_DIVIDES_NOT > 0 and t == Q - 1:
+                        nc.vector.tensor_scalar(out=result[:, v, :], in0=products[b][t][:], scalar1=scale,
+                                                scalar2=None, op0=ALU.mult)
+                    else:
+                        nc.scalar.activation(out=result[:, v, :], in_=products[b][t][:], func=ACT.Copy, scale=scale)
+                    if last:
+                        nc.sync.dma_start(out=out_quarters[b][:, t, :], in_=result[:, v, :])
+                if not last:
+                    nc.sync.dma_start(out=out_quarters[b][:, 2 * half:2 * half + 2, :], in_=result[:])
 
-        for b in range(SEQS + 1):
-            if b < SEQS:
-                scalar_mean(b)
-            if b >= 1:
-                scalar_squares(b - 1)
-        for b in range(SCALAR_REGROUPS):
+        scalar_quarters = []
+        for b in range(SEQS):
+            scalar_quarters.extend([(b, 2), (b, 3)] if b >= SCALAR_TAKES_TWO else [(b, 3)])
+        scalar_mean(*scalar_quarters[0])
+        for n in range(1, len(scalar_quarters)):
+            scalar_mean(*scalar_quarters[n])
+            scalar_squares(*scalar_quarters[n - 1])
+        scalar_squares(*scalar_quarters[-1])
+        for b in range(TENSOR_REGROUPS):
             regroup_feature(b)
+        nc.vector.memset(stats[:, SCALAR_TAKES_TWO:, 2, :], 0.0)
         for b in range(SEQS):
             for t in range(VECTOR_VARIANCES):
-                nc.vector.bn_stats(out=stats[:, b, t, :], in_=feature_in[b][:, t, :])
+                if (b, t) not in scalar_quarters:
+                    nc.vector.bn_stats(out=stats[:, b, t, :], in_=feature_in[b][:, t, :])
 
         all_minima = product_banks.tile([P, P], F32, name="all_minima", tag="product")
-        chain = [
-            lambda: nc.vector.tensor_tensor(out=mean_gap[:], in0=stats[:, :, :, 1], in1=stats[:, :, :, 4], op=ALU.subtract),
-            lambda: nc.vector.scalar_tensor_tensor(out=m2_even_odd[:], in0=stats[:, :, :, 2], scalar=EPS * (W - 1),
-                                                   in1=stats[:, :, :, 5], op0=ALU.add, op1=ALU.add),
-            lambda: nc.vector.scalar_tensor_tensor(out=gap_term[:], in0=mean_gap[:], scalar=float(W // 4),
-                                                   in1=mean_gap[:], op0=ALU.mult, op1=ALU.mult),
-            lambda: nc.vector.tensor_scalar(out=spread[:, :, VECTOR_VARIANCES], in0=scalar_m2[:], scalar1=EPS * (W - 1),
-                                            scalar2=None, op0=ALU.add),
-            lambda: nc.vector.tensor_tensor(out=spread[:, :, 0:VECTOR_VARIANCES], in0=gap_term[:], in1=m2_even_odd[:],
-                                            op=ALU.add),
-            lambda: nc.vector.tensor_reduce(out=partition_min[:], in_=spread[:], axis=AX.XY, op=ALU.min),
-            lambda: nc.tensor.transpose(all_minima[:], partition_min[:].to_broadcast([P, P]), identity_f32[:]),
-            lambda: nc.vector.reciprocal(out=inv_spread[:], in_=spread[:]),
-            lambda: nc.vector.tensor_reduce(out=global_min[:], in_=all_minima[:], axis=AX.X, op=ALU.min),
-            lambda: nc.vector.tensor_scalar(out=stability[:], in0=inv_spread[:], scalar1=global_min[:, 0:1],
-                                            scalar2=None, op0=ALU.mult),
-        ]
-        first_maxima = row_max_steps(0)
-        weave(chain, first_maxima[:-1])
-        first_maxima[-1]()
+        left_fold, right_fold, fold_2, fold_3, fold_4, row_maxima, biases = row_max_steps(0)
+        nc.vector.tensor_tensor(out=mean_gap[:], in0=stats[:, :, :, 1], in1=stats[:, :, :, 4], op=ALU.subtract)
+        nc.vector.scalar_tensor_tensor(out=m2_even_odd[:], in0=stats[:, :, :, 2], scalar=EPS * (W - 1),
+                                       in1=stats[:, :, :, 5], op0=ALU.add, op1=ALU.add)
+        nc.vector.tensor_scalar(out=spread[:, :, 3], in0=scalar_m2[:, :, 1], scalar1=EPS * (W - 1),
+                                scalar2=None, op0=ALU.add)
+        nc.vector.scalar_tensor_tensor(out=gap_term[:], in0=mean_gap[:], scalar=float(W // 4),
+                                       in1=mean_gap[:], op0=ALU.mult, op1=ALU.mult)
+        left_fold()
+        nc.vector.tensor_tensor(out=spread[:, :, 0:VECTOR_VARIANCES], in0=gap_term[:], in1=m2_even_odd[:], op=ALU.add)
+        right_fold()
+        nc.vector.tensor_scalar(out=spread[:, SCALAR_TAKES_TWO:, 2], in0=scalar_m2[:, SCALAR_TAKES_TWO:, 0],
+                                scalar1=EPS * (W - 1), scalar2=None, op0=ALU.add)
+        nc.vector.tensor_reduce(out=partition_min[:], in_=spread[:], axis=AX.XY, op=ALU.min)
+        nc.tensor.transpose(all_minima[:], partition_min[:].to_broadcast([P, P]), identity_f32[:])
+        nc.vector.reciprocal(out=inv_spread[:], in_=spread[:])
+        fold_2()
+        nc.vector.tensor_reduce(out=global_min[:], in_=all_minima[:], axis=AX.X, op=ALU.min)
+        fold_3()
+        nc.vector.tensor_scalar(out=stability[:], in0=inv_spread[:], scalar1=global_min[:, 0:1],
+                                scalar2=None, op0=ALU.mult)
+        fold_4()
+        row_maxima()
+        biases()
 
         maxima = []
         for i in range(-2, SEQS + 1):
@@ -262,8 +281,9 @@ def tile_frameaugment_t_kernel(tc, feature, noise, out):
                 others.append(lambda: quantise_feature(i + 1))
             if 0 <= i < SEQS:
                 others.append(lambda: quantise_e(i))
-                others.append(lambda: invert_row_sums(i))
-            if SCALAR_REGROUPS <= i + 3 < SEQS:
+            if i % 2 == 0 and 0 <= i < SEQS:
+                others.append(lambda: invert_row_sums(i // 2))
+            if TENSOR_REGROUPS <= i + 3 < SEQS:
                 others.append(lambda: regroup_feature(i + 3))
             weave(maxima, others)
             if i >= 1:

@@ -116,10 +116,9 @@ def tile_frameaugment_t_kernel(tc, feature, noise, out):
                 for half, pool, tag in ((0, transposed_banks, "e_transposed"), (1, product_banks, "product")):
                     cols = slice(W // 2 * half, W // 2 * (half + 1))
                     bank = pool.tile([P, W // 2, Q], BF16, name="regrouped", tag=tag)
-                    for n in range(2):
-                        nc.tensor.matmul(bank[:, P * n:P * n + P, :], lhsT=identity_bf16[:],
-                                         rhs=feature_in[b][:, :, P * (2 * half + n):P * (2 * half + n + 1)].rearrange("p k f -> p f k"),
-                                         start=True, stop=True)
+                    for pair in (slice(0, 2), slice(2, 4)):
+                        nc.tensor.matmul(bank[:, :, pair].rearrange("p f k -> p k f"), lhsT=identity_bf16[:],
+                                         rhs=feature_in[b][:, pair, cols], start=True, stop=True)
                     nc.scalar.copy(out=grouped[:, cols, :], in_=bank[:])
             else:
                 nc.vector.tensor_copy(out=grouped[:].rearrange("p (c i) t -> p c t i", i=4),

@@ -22,9 +22,11 @@ EPS = 1e-6
 STATS = 6
 
 VECTOR_VARIANCES = 3
-SCALAR_TAKES_TWO = 12
-GPSIMD_REGROUPS = 9
-TENSOR_REGROUPS = 14
+SCALAR_TAKES_TWO = 13
+EARLY_SEQS = 15
+TENSOR_SEQS = tuple(b for b in range(EARLY_SEQS) if b % 5 in (1, 3))
+GPSIMD_SEQS = tuple(b for b in range(EARLY_SEQS) if b not in TENSOR_SEQS)
+COPY_LAG = 2
 VECTOR_DIVIDES_NOT = 4
 
 
@@ -44,7 +46,7 @@ def tile_frameaugment_t_kernel(tc, feature, noise, out):
     with ExitStack() as ctx:
         ctx.enter_context(tc.manual_schedule())
         keep = ctx.enter_context(tc.tile_pool(name="keep", bufs=1))
-        inputs = ctx.enter_context(tc.tile_pool(name="inputs", bufs=SEQS + SEQS - TENSOR_REGROUPS))
+        inputs = ctx.enter_context(tc.tile_pool(name="inputs", bufs=SEQS + SEQS - EARLY_SEQS))
         work = ctx.enter_context(tc.tile_pool(name="work", bufs=2))
         transposed_banks = ctx.enter_context(tc.psum_pool(name="transposed_banks", bufs=4))
         product_banks = ctx.enter_context(tc.psum_pool(name="product_banks", bufs=Q))
@@ -107,12 +109,12 @@ def tile_frameaugment_t_kernel(tc, feature, noise, out):
 
         def regroup_feature(b):
             grouped = work.tile([P, W, Q], BF16, name="feature_grouped", tag="feature_grouped", align_bytes=64,
-                                bufs=TENSOR_REGROUPS)
+                                bufs=EARLY_SEQS)
             feature_grouped[b] = grouped
-            if b < GPSIMD_REGROUPS:
+            if b in GPSIMD_SEQS:
                 nc.gpsimd.tensor_scalar(out=grouped[:], in0=feature_in[b][:].rearrange("p t f -> p f t"),
                                         scalar1=1.0, scalar2=0.0, op0=ALU.mult, op1=ALU.add)
-            elif b < TENSOR_REGROUPS:
+            elif b in TENSOR_SEQS:
                 for half, pool, tag in ((0, transposed_banks, "e_transposed"), (1, product_banks, "product")):
                     cols = slice(W // 2 * half, W // 2 * (half + 1))
                     bank = pool.tile([P, W // 2, Q], BF16, name="regrouped", tag=tag)
@@ -217,16 +219,19 @@ def tile_frameaugment_t_kernel(tc, feature, noise, out):
                 if not last:
                     nc.sync.dma_start(out=out_quarters[b][:, 2 * half:2 * half + 2, :], in_=result[:])
 
+        for b in GPSIMD_SEQS:
+            regroup_feature(b)
         scalar_quarters = []
         for b in range(SEQS):
             scalar_quarters.extend([(b, 2), (b, 3)] if b >= SCALAR_TAKES_TWO else [(b, 3)])
-        scalar_mean(*scalar_quarters[0])
-        for n in range(1, len(scalar_quarters)):
-            scalar_mean(*scalar_quarters[n])
-            scalar_squares(*scalar_quarters[n - 1])
+        for n, (b, t) in enumerate(scalar_quarters):
+            scalar_mean(b, t)
+            if n >= 1:
+                scalar_squares(*scalar_quarters[n - 1])
+            if t == 3 and b - COPY_LAG in TENSOR_SEQS:
+                regroup_feature(b - COPY_LAG)
         scalar_squares(*scalar_quarters[-1])
-        for b in range(TENSOR_REGROUPS):
-            regroup_feature(b)
+
         nc.vector.memset(stats[:, SCALAR_TAKES_TWO:, 2, :], 0.0)
         for b in range(SEQS):
             for t in range(VECTOR_VARIANCES):
@@ -282,7 +287,7 @@ def tile_frameaugment_t_kernel(tc, feature, noise, out):
                 others.append(lambda: quantise_e(i))
             if i % 2 == 0 and 0 <= i < SEQS:
                 others.append(lambda: invert_row_sums(i // 2))
-            if TENSOR_REGROUPS <= i + 3 < SEQS:
+            if EARLY_SEQS <= i + 3 < SEQS:
                 others.append(lambda: regroup_feature(i + 3))
             weave(maxima, others)
             if i >= 1:

@@ -26,7 +26,7 @@ SCALAR_TAKES_TWO = 13
 EARLY_SEQS = 15
 TENSOR_SEQS = tuple(b for b in range(EARLY_SEQS) if b % 5 in (1, 3))
 GPSIMD_SEQS = tuple(b for b in range(EARLY_SEQS) if b not in TENSOR_SEQS)
-COPY_LAG = 2
+FULL_BANKS = 4
 VECTOR_DIVIDES_NOT = 4
 
 
@@ -228,9 +228,9 @@ def tile_frameaugment_t_kernel(tc, feature, noise, out):
             scalar_mean(b, t)
             if n >= 1:
                 scalar_squares(*scalar_quarters[n - 1])
-            if t == 3 and b - COPY_LAG in TENSOR_SEQS:
-                regroup_feature(b - COPY_LAG)
         scalar_squares(*scalar_quarters[-1])
+        for b in TENSOR_SEQS[:FULL_BANKS]:
+            regroup_feature(b)
 
         nc.vector.memset(stats[:, SCALAR_TAKES_TWO:, 2, :], 0.0)
         for b in range(SEQS):
@@ -254,6 +254,8 @@ def tile_frameaugment_t_kernel(tc, feature, noise, out):
                                 scalar1=EPS * (W - 1), scalar2=None, op0=ALU.add)
         nc.vector.tensor_reduce(out=partition_min[:], in_=spread[:], axis=AX.XY, op=ALU.min)
         nc.tensor.transpose(all_minima[:], partition_min[:].to_broadcast([P, P]), identity_f32[:])
+        for b in TENSOR_SEQS[FULL_BANKS:]:
+            regroup_feature(b)
         nc.vector.reciprocal(out=inv_spread[:], in_=spread[:])
         fold_2()
         nc.vector.tensor_reduce(out=global_min[:], in_=all_minima[:], axis=AX.X, op=ALU.min)

@@ -24,9 +24,10 @@ STATS = 6
 VECTOR_VARIANCES = 3
 SCALAR_TAKES_TWO = 13
 EARLY_SEQS = 15
-TENSOR_SEQS = tuple(b for b in range(EARLY_SEQS) if b % 5 in (1, 3))
+TENSOR_SEQS = tuple(range(1, 13, 2))
 GPSIMD_SEQS = tuple(b for b in range(EARLY_SEQS) if b not in TENSOR_SEQS)
-FULL_BANKS = 4
+COPIES_AFTER = {8: TENSOR_SEQS[0], 11: TENSOR_SEQS[1]}
+LATE_COPIES = TENSOR_SEQS[2:]
 VECTOR_DIVIDES_NOT = 4
 
 
@@ -228,8 +229,10 @@ def tile_frameaugment_t_kernel(tc, feature, noise, out):
             scalar_mean(b, t)
             if n >= 1:
                 scalar_squares(*scalar_quarters[n - 1])
+            if b in COPIES_AFTER:
+                regroup_feature(COPIES_AFTER[b])
         scalar_squares(*scalar_quarters[-1])
-        for b in TENSOR_SEQS[:FULL_BANKS]:
+        for b in LATE_COPIES:
             regroup_feature(b)
 
         nc.vector.memset(stats[:, SCALAR_TAKES_TWO:, 2, :], 0.0)
@@ -243,19 +246,17 @@ def tile_frameaugment_t_kernel(tc, feature, noise, out):
         nc.vector.tensor_tensor(out=mean_gap[:], in0=stats[:, :, :, 1], in1=stats[:, :, :, 4], op=ALU.subtract)
         nc.vector.scalar_tensor_tensor(out=m2_even_odd[:], in0=stats[:, :, :, 2], scalar=EPS * (W - 1),
                                        in1=stats[:, :, :, 5], op0=ALU.add, op1=ALU.add)
-        nc.vector.tensor_scalar(out=spread[:, :, 3], in0=scalar_m2[:, :, 1], scalar1=EPS * (W - 1),
-                                scalar2=None, op0=ALU.add)
         nc.vector.scalar_tensor_tensor(out=gap_term[:], in0=mean_gap[:], scalar=float(W // 4),
                                        in1=mean_gap[:], op0=ALU.mult, op1=ALU.mult)
         left_fold()
         nc.vector.tensor_tensor(out=spread[:, :, 0:VECTOR_VARIANCES], in0=gap_term[:], in1=m2_even_odd[:], op=ALU.add)
         right_fold()
+        nc.vector.tensor_scalar(out=spread[:, :, 3], in0=scalar_m2[:, :, 1], scalar1=EPS * (W - 1),
+                                scalar2=None, op0=ALU.add)
         nc.vector.tensor_scalar(out=spread[:, SCALAR_TAKES_TWO:, 2], in0=scalar_m2[:, SCALAR_TAKES_TWO:, 0],
                                 scalar1=EPS * (W - 1), scalar2=None, op0=ALU.add)
         nc.vector.tensor_reduce(out=partition_min[:], in_=spread[:], axis=AX.XY, op=ALU.min)
         nc.tensor.transpose(all_minima[:], partition_min[:].to_broadcast([P, P]), identity_f32[:])
-        for b in TENSOR_SEQS[FULL_BANKS:]:
-            regroup_feature(b)
         nc.vector.reciprocal(out=inv_spread[:], in_=spread[:])
         fold_2()
         nc.vector.tensor_reduce(out=global_min[:], in_=all_minima[:], axis=AX.X, op=ALU.min)

@@ -28,7 +28,11 @@ TENSOR_SEQS = tuple(range(1, 13, 2))
 GPSIMD_SEQS = tuple(b for b in range(EARLY_SEQS) if b not in TENSOR_SEQS)
 COPIES_AFTER = {8: TENSOR_SEQS[0], 11: TENSOR_SEQS[1]}
 LATE_COPIES = TENSOR_SEQS[2:]
-VECTOR_DIVIDES_NOT = 4
+TAIL_SEQ = 13
+
+
+def vector_divides(b, t):
+    return t == 3 and b < TAIL_SEQ or b == SEQS - 1 and t % 2 == 1
 
 
 def weave(first, second):
@@ -210,7 +214,7 @@ def tile_frameaugment_t_kernel(tc, feature, noise, out):
                 for v in range(2):
                     t = 2 * half + v
                     scale = inv_row_sum[b // 2][:, b % 2, t:t + 1]
-                    if v == 1 if last else b % VECTOR_DIVIDES_NOT > 0 and t == Q - 1:
+                    if vector_divides(b, t):
                         nc.vector.tensor_scalar(out=result[:, v, :], in0=products[b][t][:], scalar1=scale,
                                                 scalar2=None, op0=ALU.mult)
                     else:
@@ -246,25 +250,25 @@ def tile_frameaugment_t_kernel(tc, feature, noise, out):
         nc.vector.tensor_tensor(out=mean_gap[:], in0=stats[:, :, :, 1], in1=stats[:, :, :, 4], op=ALU.subtract)
         nc.vector.scalar_tensor_tensor(out=m2_even_odd[:], in0=stats[:, :, :, 2], scalar=EPS * (W - 1),
                                        in1=stats[:, :, :, 5], op0=ALU.add, op1=ALU.add)
+        left_fold()
         nc.vector.scalar_tensor_tensor(out=gap_term[:], in0=mean_gap[:], scalar=float(W // 4),
                                        in1=mean_gap[:], op0=ALU.mult, op1=ALU.mult)
-        left_fold()
-        nc.vector.tensor_tensor(out=spread[:, :, 0:VECTOR_VARIANCES], in0=gap_term[:], in1=m2_even_odd[:], op=ALU.add)
         right_fold()
+        nc.vector.tensor_tensor(out=spread[:, :, 0:VECTOR_VARIANCES], in0=gap_term[:], in1=m2_even_odd[:], op=ALU.add)
         nc.vector.tensor_scalar(out=spread[:, :, 3], in0=scalar_m2[:, :, 1], scalar1=EPS * (W - 1),
                                 scalar2=None, op0=ALU.add)
         nc.vector.tensor_scalar(out=spread[:, SCALAR_TAKES_TWO:, 2], in0=scalar_m2[:, SCALAR_TAKES_TWO:, 0],
                                 scalar1=EPS * (W - 1), scalar2=None, op0=ALU.add)
+        fold_2()
         nc.vector.tensor_reduce(out=partition_min[:], in_=spread[:], axis=AX.XY, op=ALU.min)
         nc.tensor.transpose(all_minima[:], partition_min[:].to_broadcast([P, P]), identity_f32[:])
         nc.vector.reciprocal(out=inv_spread[:], in_=spread[:])
-        fold_2()
-        nc.vector.tensor_reduce(out=global_min[:], in_=all_minima[:], axis=AX.X, op=ALU.min)
         fold_3()
+        fold_4()
+        nc.vector.tensor_reduce(out=global_min[:], in_=all_minima[:], axis=AX.X, op=ALU.min)
+        row_maxima()
         nc.vector.tensor_scalar(out=stability[:], in0=inv_spread[:], scalar1=global_min[:, 0:1],
                                 scalar2=None, op0=ALU.mult)
-        fold_4()
-        row_maxima()
         biases()
 
         maxima = []

from contextlib import ExitStack

import concourse.mybir as mybir
from concourse.masks import make_identity

FLOPS = 2 * 16 * 512 * 512 * 512

BF16 = mybir.dt.bfloat16
F32 = mybir.dt.float32
U32 = mybir.dt.uint32
U8 = mybir.dt.uint8
FP8X4 = mybir.dt.float8_e4m3fn_x4
ALU = mybir.AluOpType
ACT = mybir.ActivationFunctionType
AX = mybir.AxisListType

P = 128
SEQS = 16
Q = 4
W = 512
EPS = 1e-6
STATS = 6

VECTOR_VARIANCES = 3
SCALAR_TAKES_TWO = 13
EARLY_SEQS = 15
TENSOR_SEQS = tuple(range(1, 13, 2))
GPSIMD_SEQS = tuple(b for b in range(EARLY_SEQS) if b not in TENSOR_SEQS)
COPIES_AFTER = {8: TENSOR_SEQS[0], 11: TENSOR_SEQS[1]}
LATE_COPIES = TENSOR_SEQS[2:]
TAIL_SEQ = 13


def vector_divides(b, t):
    return t == 3 and b < TAIL_SEQ or b == SEQS - 1 and t % 2 == 1


def weave(first, second):
    for n in range(max(len(first), len(second))):
        for steps in (first, second):
            if n < len(steps):
                steps[n]()


def tile_frameaugment_t_kernel(tc, feature, noise, out):
    nc = tc.nc
    feature_quarters = feature.rearrange("b (p t) f -> b p t f", p=P)
    noise_quarters = noise.rearrange("b (p t) j -> b p t j", p=P)
    out_quarters = out.rearrange("b (p t) f -> b p t f", p=P)

    with ExitStack() as ctx:
        ctx.enter_context(tc.manual_schedule())
        keep = ctx.enter_context(tc.tile_pool(name="keep", bufs=1))
        inputs = ctx.enter_context(tc.tile_pool(name="inputs", bufs=SEQS + SEQS - EARLY_SEQS))
        work = ctx.enter_context(tc.tile_pool(name="work", bufs=2))
        transposed_banks = ctx.enter_context(tc.psum_pool(name="transposed_banks", bufs=4))
        product_banks = ctx.enter_context(tc.psum_pool(name="product_banks", bufs=Q))

        feature_in = [inputs.tile([P, Q, W], BF16, name="feature_in%d" % b, tag="inputs") for b in range(SEQS)]
        for t in (0, Q - 1, 1, 2):
            nc.sync.dma_start(out=feature_in[0][:, t, :], in_=feature_quarters[0][:, t, :])
        for b in range(1, SEQS):
            nc.sync.dma_start(out=feature_in[b][:], in_=feature_quarters[b])
        noise_in = []
        for b in range(SEQS):
            tile_in = inputs.tile([P, Q, W], BF16, name="noise_in%d" % b, tag="inputs")
            nc.sync.dma_start(out=tile_in[:], in_=noise_quarters[b])
            noise_in.append(tile_in)

        zero = keep.tile([P, 1], F32)
        nc.vector.memset(zero[:], 0.0)
        one = keep.tile([P, 1], F32)
        nc.scalar.activation(out=one[:], in_=zero[:], func=ACT.Exp)
        identity_f32 = keep.tile([P, P], F32)
        make_identity(nc, identity_f32[:])
        identity_bf16 = keep.tile([P, P], BF16)
        make_identity(nc, identity_bf16[:])

        stats = keep.tile([P, SEQS, VECTOR_VARIANCES, STATS], F32)
        neg_means = keep.tile([P, SEQS, 2], F32)
        scalar_m2 = keep.tile([P, SEQS, 2], F32)
        mean_gap = keep.tile([P, SEQS, VECTOR_VARIANCES], F32)
        gap_term = keep.tile([P, SEQS, VECTOR_VARIANCES], F32)
        m2_even_odd = keep.tile([P, SEQS, VECTOR_VARIANCES], F32)
        spread = keep.tile([P, SEQS, Q], F32)
        inv_spread = keep.tile([P, SEQS, Q], F32)
        stability = keep.tile([P, SEQS, Q], F32)
        partition_min = keep.tile([P, 1], F32)
        global_min = keep.tile([P, 1], F32)
        row_max = [keep.tile([P, 2, Q], F32, name="row_max%d" % n) for n in range(SEQS // 2)]
        exp_bias = [keep.tile([P, 2, Q], F32, name="exp_bias%d" % n) for n in range(SEQS // 2)]
        row_sum = [keep.tile([P, 2, Q], F32, name="row_sum%d" % n) for n in range(SEQS // 2)]
        inv_row_sum = [keep.tile([P, 2, Q], F32, name="inv_row_sum%d" % n) for n in range(SEQS // 2)]
        feature_codes = [keep.tile([P, W], U32, name="feature_codes%d" % b, align_bytes=64) for b in range(SEQS)]
        feature_scales = [keep.tile([P, W], U8, name="feature_scales%d" % b, align_bytes=64) for b in range(SEQS)]

        feature_grouped = {}
        e_rows = {}
        e_transposed = {}
        e_grouped = {}
        e_quantised = {}
        products = {}


        def scalar_mean(b, t):
            unused = work.tile([P, W], BF16, name="unused", tag="unused")
            nc.scalar.activation(out=unused[:], in_=feature_in[b][:, t, :], func=ACT.Copy,
                                 scale=-1.0 / W, accum_out=neg_means[:, b, t - 2:t - 1])

        def scalar_squares(b, t):
            unused = work.tile([P, W], BF16, name="unused", tag="unused")
            nc.scalar.activation(out=unused[:], in_=feature_in[b][:, t, :], func=ACT.Square,
                                 bias=neg_means[:, b, t - 2:t - 1], accum_out=scalar_m2[:, b, t - 2:t - 1])

        def regroup_feature(b):
            grouped = work.tile([P, W, Q], BF16, name="feature_grouped", tag="feature_grouped", align_bytes=64,
                                bufs=EARLY_SEQS)
            feature_grouped[b] = grouped
            if b in GPSIMD_SEQS:
                nc.gpsimd.tensor_scalar(out=grouped[:], in0=feature_in[b][:].rearrange("p t f -> p f t"),
                                        scalar1=1.0, scalar2=0.0, op0=ALU.mult, op1=ALU.add)
            elif b in TENSOR_SEQS:
                for half, pool, tag in ((0, transposed_banks, "e_transposed"), (1, product_banks, "product")):
                    cols = slice(W // 2 * half, W // 2 * (half + 1))
                    bank = pool.tile([P, W // 2, Q], BF16, name="regrouped", tag=tag)
                    for pair in (slice(0, 2), slice(2, 4)):
                        nc.tensor.matmul(bank[:, :, pair].rearrange("p f k -> p k f"), lhsT=identity_bf16[:],
                                         rhs=feature_in[b][:, pair, cols], start=True, stop=True)
                    nc.scalar.copy(out=grouped[:, cols, :], in_=bank[:])
            else:
                nc.vector.tensor_copy(out=grouped[:].rearrange("p (c i) t -> p c t i", i=4),
                                      in_=feature_in[b][:].rearrange("p t (c i) -> p c t i", i=4))

        def quantise_feature(b):
            nc.vector.quantize_mx(out=feature_codes[b][:].bitcast(FP8X4), scales=feature_scales[b][:],
                                  in_=feature_grouped[b][:].rearrange("p f t -> p (f t)"))

        def row_max_steps(n):
            widths = (W // 2, W // 4, W // 8, W // 16)
            folded = [work.tile([P, 2, Q, w], BF16, name="folded%d" % w, tag="folded%d" % w) for w in widths]

            def first_fold(s):
                w = widths[0]
                source = noise_in[2 * n + s]
                return lambda: nc.vector.tensor_tensor(out=folded[0][:, s, :, :], in0=source[:, :, 0:w],
                                                       in1=source[:, :, w:2 * w], op=ALU.max)

            def fold(m):
                w = widths[m]
                both = [folded[m - 1][:].rearrange("p s t w -> p (s t) w"), folded[m][:].rearrange("p s t w -> p (s t) w")]
                return lambda: nc.vector.tensor_tensor(out=both[1], in0=both[0][:, :, 0:w],
                                                       in1=both[0][:, :, w:2 * w], op=ALU.max)

            steps = [first_fold(0), first_fold(1)]
            steps.extend([fold(m) for m in range(1, len(widths))])
            steps.append(lambda: nc.vector.tensor_reduce(out=row_max[n][:], in_=folded[-1][:], axis=AX.X, op=ALU.max))
            steps.append(lambda: nc.vector.scalar_tensor_tensor(
                out=exp_bias[n][:], in0=stability[:, 2 * n:2 * n + 2, :], scalar=-1.0, in1=row_max[n][:],
                op0=ALU.mult, op1=ALU.mult))
            return steps

        def exponentials(b):
            e_rows[b] = work.tile([P, Q, W], BF16, name="e_rows", tag="e_rows")
            for t in range(Q):
                nc.scalar.activation(out=e_rows[b][:, t, :].rearrange("p (u w h) -> p u w h", u=2, h=2),
                                     in_=noise_in[b][:, t, :].rearrange("p (w u h) -> p u w h", u=2, h=2), func=ACT.Exp,
                                     bias=exp_bias[b // 2][:, b % 2, t:t + 1], scale=stability[:, b, t:t + 1],
                                     accum_out=row_sum[b // 2][:, b % 2, t:t + 1])

        def transposes(b):
            words = e_rows[b][:].rearrange("p t j -> p (t j)").bitcast(F32)
            e_transposed[b] = []
            for half in range(2):
                bank = transposed_banks.tile([P, 2, 2, P], F32, name="e_transposed", tag="e_transposed")
                for v in range(2):
                    for u in range(2):
                        run = (2 * half + v) * 2 + u
                        nc.tensor.transpose(bank[:, v, u, :], words[:, P * run:P * run + P], identity_f32[:])
                e_transposed[b].append(bank)

        def regroup_e(b, half):
            if half == 0:
                e_grouped[b] = work.tile([P, Q, P, Q], BF16, name="e_grouped", tag="e_grouped", align_bytes=64)
            words = e_grouped[b][:].rearrange("p t i k -> p (t i k)").bitcast(F32)
            words = words.rearrange("p (t i u) -> p t i u", t=Q, u=2)
            nc.vector.tensor_copy(out=words[:, 2 * half:2 * half + 2, :, :],
                                  in_=e_transposed[b][half][:].rearrange("p v u i -> p v i u"))

        def quantise_e(b):
            codes = work.tile([P, W], U32, name="e_codes", tag="e_codes", align_bytes=64)
            scales = work.tile([P, W], U8, name="e_scales", tag="e_scales", align_bytes=64)
            e_quantised[b] = (codes, scales)
            nc.vector.quantize_mx(out=codes[:].bitcast(FP8X4), scales=scales[:],
                                  in_=e_grouped[b][:].rearrange("p t i k -> p (t i k)"))

        def invert_row_sums(n):
            nc.vector.reciprocal(out=inv_row_sum[n][:], in_=row_sum[n][:])

        def multiply(b):
            codes, scales = e_quantised[b]
            products[b] = []
            for t in range(Q):
                bank = product_banks.tile([P, W], F32, name="product", tag="product")
                nc.tensor.matmul_mx(out=bank[:], lhsT=codes[:, P * t:P * t + P].bitcast(FP8X4),
                                    lhsT_scale=scales[:, P * t:P * t + P],
                                    rhs=feature_codes[b][:].bitcast(FP8X4), rhs_scale=feature_scales[b][:],
                                    start=True, stop=True)
                products[b].append(bank)

        def divide_and_store(b):
            last = b == SEQS - 1
            for half in range(2):
                result = work.tile([P, 2, W], F32, name="result", tag="result", bufs=6)
                for v in range(2):
                    t = 2 * half + v
                    scale = inv_row_sum[b // 2][:, b % 2, t:t + 1]
                    if vector_divides(b, t):
                        nc.vector.tensor_scalar(out=result[:, v, :], in0=products[b][t][:], scalar1=scale,
                                                scalar2=None, op0=ALU.mult)
                    else:
                        nc.scalar.activation(out=result[:, v, :], in_=products[b][t][:], func=ACT.Copy, scale=scale)
                    if last:
                        nc.sync.dma_start(out=out_quarters[b][:, t, :], in_=result[:, v, :])
                if not last:
                    nc.sync.dma_start(out=out_quarters[b][:, 2 * half:2 * half + 2, :], in_=result[:])

        for b in GPSIMD_SEQS:
            regroup_feature(b)
        scalar_quarters = []
        for b in range(SEQS):
            scalar_quarters.extend([(b, 2), (b, 3)] if b >= SCALAR_TAKES_TWO else [(b, 3)])
        for n, (b, t) in enumerate(scalar_quarters):
            scalar_mean(b, t)
            if n >= 1:
                scalar_squares(*scalar_quarters[n - 1])
            if b in COPIES_AFTER:
                regroup_feature(COPIES_AFTER[b])
        scalar_squares(*scalar_quarters[-1])
        for b in LATE_COPIES:
            regroup_feature(b)

        nc.vector.memset(stats[:, SCALAR_TAKES_TWO:, 2, :], 0.0)
        for b in range(SEQS):
            for t in range(VECTOR_VARIANCES):
                if (b, t) not in scalar_quarters:
                    nc.vector.bn_stats(out=stats[:, b, t, :], in_=feature_in[b][:, t, :])

        all_minima = product_banks.tile([P, P], F32, name="all_minima", tag="product")
        left_fold, right_fold, fold_2, fold_3, fold_4, row_maxima, biases = row_max_steps(0)
        nc.vector.tensor_tensor(out=mean_gap[:], in0=stats[:, :, :, 1], in1=stats[:, :, :, 4], op=ALU.subtract)
        nc.vector.scalar_tensor_tensor(out=m2_even_odd[:], in0=stats[:, :, :, 2], scalar=EPS * (W - 1),
                                       in1=stats[:, :, :, 5], op0=ALU.add, op1=ALU.add)
        left_fold()
        nc.vector.scalar_tensor_tensor(out=gap_term[:], in0=mean_gap[:], scalar=float(W // 4),
                                       in1=mean_gap[:], op0=ALU.mult, op1=ALU.mult)
        right_fold()
        nc.vector.tensor_tensor(out=spread[:, :, 0:VECTOR_VARIANCES], in0=gap_term[:], in1=m2_even_odd[:], op=ALU.add)
        nc.vector.tensor_scalar(out=spread[:, :, 3], in0=scalar_m2[:, :, 1], scalar1=EPS * (W - 1),
                                scalar2=None, op0=ALU.add)
        nc.vector.tensor_scalar(out=spread[:, SCALAR_TAKES_TWO:, 2], in0=scalar_m2[:, SCALAR_TAKES_TWO:, 0],
                                scalar1=EPS * (W - 1), scalar2=None, op0=ALU.add)
        fold_2()
        nc.vector.tensor_reduce(out=partition_min[:], in_=spread[:], axis=AX.XY, op=ALU.min)
        nc.tensor.transpose(all_minima[:], partition_min[:].to_broadcast([P, P]), identity_f32[:])
        nc.vector.reciprocal(out=inv_spread[:], in_=spread[:])
        fold_3()
        fold_4()
        nc.vector.tensor_reduce(out=global_min[:], in_=all_minima[:], axis=AX.X, op=ALU.min)
        row_maxima()
        nc.vector.tensor_scalar(out=stability[:], in0=inv_spread[:], scalar1=global_min[:, 0:1],
                                scalar2=None, op0=ALU.mult)
        biases()

        maxima = []
        for i in range(-2, SEQS + 1):
            if i + 2 < SEQS:
                exponentials(i + 2)
            if 0 <= i + 1 < SEQS:
                transposes(i + 1)
            if i >= 1:
                multiply(i - 1)
            if i % 2 == 0:
                steps = row_max_steps(i // 2 + 2) if i + 4 < SEQS else []
                maxima, later = steps[:3], steps[3:]
            else:
                maxima = later
            others = []
            if 0 <= i < SEQS:
                others.append(lambda: regroup_e(i, 0))
                others.append(lambda: regroup_e(i, 1))
            if 0 <= i + 1 < SEQS:
                others.append(lambda: quantise_feature(i + 1))
            if 0 <= i < SEQS:
                others.append(lambda: quantise_e(i))
            if i % 2 == 0 and 0 <= i < SEQS:
                others.append(lambda: invert_row_sums(i // 2))
            if EARLY_SEQS <= i + 3 < SEQS:
                others.append(lambda: regroup_feature(i + 3))
            weave(maxima, others)
            if i >= 1:
                divide_and_store(i - 1)
